import numpy as np
import ml_dtypes


def mxq(x, axis, fmt="e4m3"):
    dtype, down = {"e4m3": (ml_dtypes.float8_e4m3fn, 7), "e5m2": (ml_dtypes.float8_e5m2, 14)}[fmt]
    v = np.moveaxis(np.asarray(x, np.float32).astype(ml_dtypes.bfloat16).astype(np.float64), axis, -1)
    blocks = v.reshape(v.shape[:-1] + (-1, 32))
    amax = np.abs(blocks).max(-1, keepdims=True)
    byte = np.maximum(np.where(amax > 0, np.frexp(amax)[1] - 1 + 127, 0) - down, 1)
    scale = np.exp2(byte - 127.0)
    codes = (blocks / scale).astype(np.float32).astype(dtype).astype(np.float64)
    return np.moveaxis((codes * scale).reshape(v.shape), -1, axis)


WIDE = False


def mx_kscale(k):
    if not WIDE:
        return np.ones(k)
    levels = np.array([10, -10, 5, -5, 0])
    if k % 512:
        return np.exp2(np.random.permutation(np.resize(levels, k // 32))).repeat(32)
    a = np.empty((k // 512, 16))
    for p in range(k // 512):
        a[p, :8] = np.random.permutation(np.resize(levels, 8))
        for g in range(8):
            far = levels[np.abs(levels - a[p, g]) >= 10]
            a[p, g + 8] = far[np.random.randint(len(far))]
    return np.exp2(a.ravel()).repeat(32)


BF16 = ml_dtypes.bfloat16


def bf(x):
    return np.asarray(x, np.float32).astype(BF16)


def f64(x):
    return np.asarray(x).astype(np.float64)


T, B, D, H, HD, A = 512, 1, 1024, 16, 128, 128
HH = H * HD
CAT = HH + D
EPS = 1e-5
AO = 0.6


def layer_norm(x, w, b):
    mu = x.mean(-1, keepdims=True)
    var = np.square(x - mu).mean(-1, keepdims=True)
    return (x - mu) * (1.0 / np.sqrt(var + EPS)) * w + b


def setup_inputs():
    t = mx_kscale(HH)
    w_out = np.random.standard_normal((CAT, D)) / np.sqrt(CAT)
    w_out[:HH] = w_out[:HH] / t[:, None]
    return {"u": bf(np.random.standard_normal((T, B, HH)) * t),
            "attn_out": bf(AO * np.random.standard_normal((T, B, HH)) * t),
            "src_norm": bf(np.random.standard_normal((T, B, D))),
            "w_out": bf(w_out),
            "b_out": bf(0.1 * np.random.standard_normal(D)),
            "ln2_w": bf(1.0 + 0.1 * np.random.standard_normal(D)),
            "ln2_b": bf(0.1 * np.random.standard_normal(D))}


def reference(u, attn_out, src_norm, w_out, b_out, ln2_w, ln2_b):
    residual = f64(u) + f64(attn_out)
    xn = f64(src_norm)
    cat = np.concatenate([residual, xn], -1)
    z = (mxq(cat, 2, "e4m3") @ mxq(f64(w_out), 0, "e4m3")) + f64(b_out)
    return layer_norm(z, f64(ln2_w), f64(ln2_b)) + xn

@@ -1,0 +1,283 @@
+from contextlib import ExitStack
+
+import concourse.mybir as mybir
+from concourse.masks import make_identity
+
+F32 = mybir.dt.float32
+BF16 = mybir.dt.bfloat16
+U32 = mybir.dt.uint32
+U8 = mybir.dt.uint8
+FP8X4 = mybir.dt.float8_e4m3fn_x4
+ALU = mybir.AluOpType
+ACT = mybir.ActivationFunctionType
+
+P = 128
+PACK = 4
+K_PASS = P * PACK
+TOKENS = 512
+RES = 2048
+D = 1024
+K = RES + D
+BANK = 512
+EPS = 1e-5
+
+TOKEN_TILES = TOKENS // P
+EARLY_TILES = 2
+PASSES = K // K_PASS
+RES_PASSES = RES // K_PASS
+HALVES = D // BANK
+LAG = 2
+PASS_ORDER = list(range(RES_PASSES, PASSES)) + list(range(RES_PASSES))
+
+FLOPS = 2 * TOKENS * K * D
+
+
+def tile_stulayer_pb_kernel(tc, u, attn_out, src_norm, w_out, b_out, ln2_w, ln2_b, out):
+    nc = tc.nc
+    u_rows = u.rearrange("t b f -> (t b) f")
+    attn_rows = attn_out.rearrange("t b f -> (t b) f")
+    src_rows = src_norm.rearrange("t b f -> (t b) f")
+    out_rows = out.rearrange("t b f -> (t b) f")
+
+    with ExitStack() as ctx:
+        keep = ctx.enter_context(tc.tile_pool(name="keep", bufs=1))
+        stage = ctx.enter_context(tc.tile_pool(name="stage", bufs=2))
+        small = ctx.enter_context(tc.tile_pool(name="small", bufs=TOKEN_TILES))
+        psum = ctx.enter_context(tc.psum_pool(name="psum", bufs=8))
+
+        vec_rows = keep.tile([P, P], BF16)
+        nc.vector.memset(vec_rows[:], 0.0)
+        nc.scalar.dma_start(out=vec_rows[0:8, :], in_=b_out.rearrange("(r c) -> r c", c=P))
+        nc.scalar.dma_start(out=vec_rows[8:16, :], in_=ln2_w.rearrange("(r c) -> r c", c=P))
+        shift_row = keep.tile([P, D], BF16)
+        nc.vector.memset(shift_row[:], 0.0)
+        nc.scalar.dma_start(out=shift_row[0:1, :], in_=ln2_b.rearrange("(o c) -> o c", o=1))
+
+        u_tiles = [keep.tile([P, RES], BF16, name="u%d" % i) for i in range(TOKEN_TILES)]
+        attn_tiles = [keep.tile([P, RES], BF16, name="attn%d" % i) for i in range(TOKEN_TILES)]
+        src_tiles = [keep.tile([P, D], BF16, name="src%d" % i) for i in range(TOKEN_TILES)]
+        w_raw = [keep.tile([P, PACK, D], BF16, name="w_raw%d" % g) for g in range(PASSES)]
+
+        def load_tokens(i):
+            rows = slice(i * P, (i + 1) * P)
+            nc.sync.dma_start(out=src_tiles[i][:], in_=src_rows[rows, :])
+            nc.sync.dma_start(out=u_tiles[i][:], in_=u_rows[rows, :])
+            nc.sync.dma_start(out=attn_tiles[i][:], in_=attn_rows[rows, :])
+
+        def load_weights(g):
+            nc.sync.dma_start(
+                out=w_raw[g][:],
+                in_=w_out[g * K_PASS : (g + 1) * K_PASS, :].rearrange("(p t) c -> p t c", t=PACK),
+            )
+
+        for n, g in enumerate(PASS_ORDER):
+            load_weights(g)
+            if n < EARLY_TILES:
+                load_tokens(n)
+        for i in range(EARLY_TILES, TOKEN_TILES):
+            load_tokens(i)
+
+        eps = keep.tile([P, 1], F32)
+        nc.vector.memset(eps[:], EPS)
+        warm = keep.tile([P, 1], F32)
+        nc.scalar.activation(out=warm[:], in_=eps[:], func=ACT.Abs_reciprocal_sqrt)
+        ident_bf16 = keep.tile([P, P], BF16)
+        make_identity(nc, ident_bf16[:])
+        ident_f32 = keep.tile([P, P], F32)
+        make_identity(nc, ident_f32[:])
+        ones = keep.tile([P, P], BF16)
+        nc.vector.memset(ones[:], 1.0)
+
+        vec_cols_ps = psum.tile([P, P], BF16, tag="bank")
+        nc.tensor.transpose(vec_cols_ps[:], vec_rows[:], ident_bf16[:])
+        vec_cols = keep.tile([P, P], BF16)
+        nc.scalar.copy(out=vec_cols[:], in_=vec_cols_ps[:])
+        bias_all = keep.tile([P, D], BF16)
+        gain_all = keep.tile([P, D], BF16)
+        for first_row, spread in ((0, bias_all), (8, gain_all)):
+            spread_ps = psum.tile([P, D], BF16, tag="bank")
+            for r in range(D // P):
+                column = vec_cols[:, first_row + r : first_row + r + 1]
+                nc.tensor.transpose(
+                    spread_ps[:, r * P : (r + 1) * P], column.to_broadcast([P, P]), ident_bf16[:]
+                )
+            nc.scalar.copy(out=spread[:], in_=spread_ps[:])
+
+        cat_codes = keep.tile([P, TOKEN_TILES, PASSES * P], U32, align_bytes=64)
+        cat_scales = keep.tile([P, TOKEN_TILES, PASSES * P], U8, align_bytes=64)
+        w_codes = keep.tile([P, PASSES, D], U32, align_bytes=64)
+        w_scales = keep.tile([P, PASSES, D], U8, align_bytes=64)
+
+        ready_tiles = []
+        ready_weights = []
+        accs = {}
+        issued = {}
+
+        def multiply(i, g, h):
+            cols = slice(h * BANK, (h + 1) * BANK)
+            nc.tensor.matmul_mx(
+                out=accs[i][h][:],
+                lhsT=cat_codes[:, i, g * P : (g + 1) * P].bitcast(FP8X4),
+                lhsT_scale=cat_scales[:, i, g * P : (g + 1) * P],
+                rhs=w_codes[:, g, cols].bitcast(FP8X4),
+                rhs_scale=w_scales[:, g, cols],
+                start=(issued[(i, h)] == 0),
+                stop=(issued[(i, h)] == PASSES - 1),
+            )
+            issued[(i, h)] = issued[(i, h)] + 1
+
+        def flip_two_passes(rows):
+            words = rows.bitcast(F32)
+            flipped = psum.tile([P, 4, P], F32, tag="bank")
+            for q in range(4):
+                g, h = divmod(q, 2)
+                every_second = words[:, 2 * P * g + h : 2 * P * (g + 1) : 2]
+                nc.tensor.transpose(flipped[:, q, :], every_second, ident_f32[:])
+            grouped = stage.tile([P, 2 * K_PASS], BF16, align_bytes=64, name="cat_grouped", bufs=6)
+            nc.scalar.copy(
+                out=grouped[:].bitcast(F32).rearrange("p (g t h) -> p g t h", t=P, h=2),
+                in_=flipped[:].rearrange("p (g h) t -> p g t h", h=2),
+            )
+            return grouped
+
+        def flip_tokens(i):
+            flips = [(RES_PASSES, flip_two_passes(src_tiles[i][:]))]
+            for first_pass in range(0, RES_PASSES, 2):
+                cols = slice(first_pass * K_PASS, (first_pass + 2) * K_PASS)
+                residual = stage.tile([P, 2 * K_PASS], BF16, bufs=4)
+                nc.vector.tensor_tensor(
+                    out=residual[:], in0=u_tiles[i][:, cols], in1=attn_tiles[i][:, cols], op=ALU.add
+                )
+                flips.append((first_pass, flip_two_passes(residual[:])))
+            return flips
+
+        def quantise_tokens(i, flips):
+            for first_pass, grouped in flips:
+                cols = slice(first_pass * P, (first_pass + 2) * P)
+                nc.vector.quantize_mx(
+                    out=cat_codes[:, i, cols].bitcast(FP8X4), scales=cat_scales[:, i, cols], in_=grouped[:]
+                )
+            accs[i] = [psum.tile([P, BANK], F32, tag="bank", name="acc%d%d" % (i, h)) for h in range(HALVES)]
+            for h in range(HALVES):
+                issued[(i, h)] = 0
+            for g, h in ready_weights:
+                multiply(i, g, h)
+            ready_tiles.append(i)
+
+        def regroup_weights(g):
+            halves = []
+            for h in range(HALVES):
+                grouped = stage.tile([P, BANK * PACK], BF16, align_bytes=64, name="w_grouped%d" % h)
+                copy = nc.vector.tensor_copy if h == 0 else nc.scalar.copy
+                copy(
+                    out=grouped[:].rearrange("p (c i t) -> p c t i", i=4, t=PACK),
+                    in_=w_raw[g][:, :, h * BANK : (h + 1) * BANK].rearrange("p t (c i) -> p c t i", i=4),
+                )
+                halves.append(grouped)
+            return halves
+
+        def quantise_weights(g, h, grouped):
+            cols = slice(h * BANK, (h + 1) * BANK)
+            nc.vector.quantize_mx(
+                out=w_codes[:, g, cols].bitcast(FP8X4), scales=w_scales[:, g, cols], in_=grouped[:]
+            )
+            for i in ready_tiles:
+                multiply(i, g, h)
+            ready_weights.append((g, h))
+
+        def centre_and_gain(i):
+            z = stage.tile([P, D], F32)
+            z_sum = small.tile([P, HALVES], F32)
+            for h in range(HALVES):
+                cols = slice(h * BANK, (h + 1) * BANK)
+                nc.vector.scalar_tensor_tensor(
+                    out=z[:, cols],
+                    in0=accs[i][h][:],
+                    scalar=1.0,
+                    in1=bias_all[:, cols],
+                    op0=ALU.mult,
+                    op1=ALU.add,
+                    accum_out=z_sum[:, h : h + 1],
+                )
+            neg_mean = small.tile([P, 1], F32)
+            nc.vector.tensor_scalar(
+                out=neg_mean[:],
+                in0=z_sum[:, 0:1],
+                scalar1=z_sum[:, 1:2],
+                scalar2=-1.0 / D,
+                op0=ALU.add,
+                op1=ALU.mult,
+            )
+            shifted = []
+            for h in range(HALVES):
+                cols = slice(h * BANK, (h + 1) * BANK)
+                shifted_ps = psum.tile([P, BANK], F32, tag="bank", name="shifted%d" % h)
+                nc.tensor.matmul(
+                    out=shifted_ps[:], lhsT=ident_bf16[:], rhs=src_tiles[i][:, cols], start=True, stop=False
+                )
+                nc.tensor.matmul(
+                    out=shifted_ps[:], lhsT=ones[:], rhs=shift_row[:, cols], start=False, stop=True
+                )
+                shifted.append(shifted_ps)
+
+            gained = stage.tile([P, D], F32, bufs=LAG + 1)
+            if i < TOKEN_TILES - 1:
+                centred = stage.tile([P, D], F32)
+                nc.scalar.activation(out=centred[:], in_=z[:], func=ACT.Identity, bias=neg_mean[:])
+                nc.gpsimd.tensor_tensor(out=gained[:], in0=centred[:], in1=gain_all[:], op=ALU.mult)
+            else:
+                nc.vector.scalar_tensor_tensor(
+                    out=gained[:], in0=z[:], scalar=neg_mean[:], in1=gain_all[:], op0=ALU.add, op1=ALU.mult
+                )
+
+            squares = stage.tile([P, D], BF16)
+            sq_sum = small.tile([P, 1], F32)
+            nc.scalar.activation(
+                out=squares[:], in_=z[:], func=ACT.Square, bias=neg_mean[:], accum_out=sq_sum[:]
+            )
+            rstd = small.tile([P, 1], F32)
+            nc.scalar.activation(
+                out=rstd[:], in_=sq_sum[:], func=ACT.Abs_reciprocal_sqrt, bias=eps[:], scale=1.0 / D
+            )
+            return gained, rstd, shifted
+
+        def scale_and_store(i, gained, rstd, shifted):
+            result = stage.tile([P, D], F32)
+            for h in range(HALVES):
+                cols = slice(h * BANK, (h + 1) * BANK)
+                nc.vector.scalar_tensor_tensor(
+                    out=result[:, cols],
+                    in0=gained[:, cols],
+                    scalar=rstd[:],
+                    in1=shifted[h][:],
+                    op0=ALU.mult,
+                    op1=ALU.add,
+                )
+                nc.sync.dma_start(out=out_rows[i * P : (i + 1) * P, cols], in_=result[:, cols])
+
+        flips = {}
+        waiting = None
+        for n, g in enumerate(PASS_ORDER):
+            halves = regroup_weights(g)
+            if waiting is not None:
+                quantise_weights(waiting[0], 1, waiting[1])
+            quantise_weights(g, 0, halves[0])
+            waiting = (g, halves[1])
+            if 0 <= n - 1 < EARLY_TILES:
+                quantise_tokens(n - 1, flips[n - 1])
+            if n < EARLY_TILES:
+                flips[n] = flip_tokens(n)
+        quantise_weights(waiting[0], 1, waiting[1])
+
+        ends = {}
+        for i in range(TOKEN_TILES):
+            late = i + EARLY_TILES
+            if late < TOKEN_TILES:
+                flips[late] = flip_tokens(late)
+            if EARLY_TILES <= late - 1 < TOKEN_TILES:
+                quantise_tokens(late - 1, flips[late - 1])
+            if i >= LAG:
+                scale_and_store(i - LAG, *ends[i - LAG])
+            ends[i] = centre_and_gain(i)
+        for i in range(TOKEN_TILES - LAG, TOKEN_TILES):
+            scale_and_store(i, *ends[i])

@@ -22,13 +22,11 @@ BANK = 512
 EPS = 1e-5
 
 TOKEN_TILES = TOKENS // P
-EARLY_TILES = 2
 PASSES = K // K_PASS
 RES_PASSES = RES // K_PASS
 HALVES = D // BANK
-LAG = 2
-PASS_ORDER = list(range(RES_PASSES, PASSES)) + list(range(RES_PASSES))
 
+SPLIT = (3, 4)
 FLOPS = 2 * TOKENS * K * D
 
 
@@ -40,68 +38,95 @@ def tile_stulayer_pb_kernel(tc, u, attn_out, src_norm, w_out, b_out, ln2_w, ln2_
     out_rows = out.rearrange("t b f -> (t b) f")
 
     with ExitStack() as ctx:
+        ctx.enter_context(tc.manual_schedule())
         keep = ctx.enter_context(tc.tile_pool(name="keep", bufs=1))
         stage = ctx.enter_context(tc.tile_pool(name="stage", bufs=2))
         small = ctx.enter_context(tc.tile_pool(name="small", bufs=TOKEN_TILES))
-        psum = ctx.enter_context(tc.psum_pool(name="psum", bufs=8))
+        psum = ctx.enter_context(tc.psum_pool(name="psum", bufs=1))
 
         vec_rows = keep.tile([P, P], BF16)
         nc.vector.memset(vec_rows[:], 0.0)
-        nc.scalar.dma_start(out=vec_rows[0:8, :], in_=b_out.rearrange("(r c) -> r c", c=P))
-        nc.scalar.dma_start(out=vec_rows[8:16, :], in_=ln2_w.rearrange("(r c) -> r c", c=P))
         shift_row = keep.tile([P, D], BF16)
         nc.vector.memset(shift_row[:], 0.0)
-        nc.scalar.dma_start(out=shift_row[0:1, :], in_=ln2_b.rearrange("(o c) -> o c", o=1))
+        eps = keep.tile([P, 1], F32)
+        nc.vector.memset(eps[:], EPS)
+        ones = keep.tile([P, P], BF16)
+        nc.vector.memset(ones[:], 1.0)
 
         u_tiles = [keep.tile([P, RES], BF16, name="u%d" % i) for i in range(TOKEN_TILES)]
         attn_tiles = [keep.tile([P, RES], BF16, name="attn%d" % i) for i in range(TOKEN_TILES)]
         src_tiles = [keep.tile([P, D], BF16, name="src%d" % i) for i in range(TOKEN_TILES)]
-        w_raw = [keep.tile([P, PACK, D], BF16, name="w_raw%d" % g) for g in range(PASSES)]
+        w_raw = [keep.tile([P, HALVES, PACK, BANK] if g in SPLIT else [P, PACK, D], BF16, name="w_raw%d" % g) for g in range(PASSES)]
 
-        def load_tokens(i):
+        def load_src(i):
+            nc.sync.dma_start(out=src_tiles[i][:], in_=src_rows[i * P : (i + 1) * P, :])
+
+        def load_residual(i, parts=1):
             rows = slice(i * P, (i + 1) * P)
-            nc.sync.dma_start(out=src_tiles[i][:], in_=src_rows[rows, :])
-            nc.sync.dma_start(out=u_tiles[i][:], in_=u_rows[rows, :])
-            nc.sync.dma_start(out=attn_tiles[i][:], in_=attn_rows[rows, :])
+            width = RES // parts
+            for c in range(parts):
+                cols = slice(c * width, (c + 1) * width)
+                nc.sync.dma_start(out=u_tiles[i][:, cols], in_=u_rows[rows, cols])
+                nc.sync.dma_start(out=attn_tiles[i][:, cols], in_=attn_rows[rows, cols])
 
-        def load_weights(g):
+        def load_w_part(g, h):
+            cols = slice(h * BANK, (h + 1) * BANK)
             nc.sync.dma_start(
-                out=w_raw[g][:],
-                in_=w_out[g * K_PASS : (g + 1) * K_PASS, :].rearrange("(p t) c -> p t c", t=PACK),
+                out=w_raw[g][:, h],
+                in_=w_out[g * K_PASS : (g + 1) * K_PASS, cols].rearrange("(p t) c -> p t c", t=PACK),
             )
 
-        for n, g in enumerate(PASS_ORDER):
-            load_weights(g)
-            if n < EARLY_TILES:
-                load_tokens(n)
-        for i in range(EARLY_TILES, TOKEN_TILES):
-            load_tokens(i)
+        def load_weights(g, parts=1):
+            width = D // parts
+            for c in range(parts):
+                cols = slice(c * width, (c + 1) * width)
+                nc.sync.dma_start(
+                    out=w_raw[g][:, :, cols],
+                    in_=w_out[g * K_PASS : (g + 1) * K_PASS, cols].rearrange("(p t) c -> p t c", t=PACK),
+                )
 
-        eps = keep.tile([P, 1], F32)
-        nc.vector.memset(eps[:], EPS)
+        load_w_part(4, 0)
+        nc.sync.dma_start(out=vec_rows[0:8, :], in_=b_out.rearrange("(r c) -> r c", c=P))
+        nc.sync.dma_start(out=vec_rows[8:16, :], in_=ln2_w.rearrange("(r c) -> r c", c=P))
+        load_w_part(4, 1)
+        load_weights(5)
+        load_src(0)
+        load_residual(0)
+        nc.sync.dma_start(out=shift_row[0:1, :], in_=ln2_b.rearrange("(o c) -> o c", o=1))
+        load_weights(0)
+        load_src(1)
+        load_residual(1)
+        load_weights(1)
+        load_src(2)
+        load_residual(2)
+        load_weights(2)
+        load_w_part(3, 0)
+        load_w_part(3, 1)
+        load_src(3)
+        load_residual(3, parts=2)
+
         warm = keep.tile([P, 1], F32)
         nc.scalar.activation(out=warm[:], in_=eps[:], func=ACT.Abs_reciprocal_sqrt)
         ident_bf16 = keep.tile([P, P], BF16)
         make_identity(nc, ident_bf16[:])
         ident_f32 = keep.tile([P, P], F32)
         make_identity(nc, ident_f32[:])
-        ones = keep.tile([P, P], BF16)
-        nc.vector.memset(ones[:], 1.0)
 
-        vec_cols_ps = psum.tile([P, P], BF16, tag="bank")
+        vec_cols_ps = psum.tile([P, P], BF16, tag="t0")
         nc.tensor.transpose(vec_cols_ps[:], vec_rows[:], ident_bf16[:])
         vec_cols = keep.tile([P, P], BF16)
         nc.scalar.copy(out=vec_cols[:], in_=vec_cols_ps[:])
         bias_all = keep.tile([P, D], BF16)
         gain_all = keep.tile([P, D], BF16)
-        for first_row, spread in ((0, bias_all), (8, gain_all)):
-            spread_ps = psum.tile([P, D], BF16, tag="bank")
+
+        def spread(first_row, target, bank):
+            spread_ps = psum.tile([P, D], BF16, tag=bank)
             for r in range(D // P):
                 column = vec_cols[:, first_row + r : first_row + r + 1]
                 nc.tensor.transpose(
                     spread_ps[:, r * P : (r + 1) * P], column.to_broadcast([P, P]), ident_bf16[:]
                 )
-            nc.scalar.copy(out=spread[:], in_=spread_ps[:])
+            nc.scalar.copy(out=target[:], in_=spread_ps[:])
 
         cat_codes = keep.tile([P, TOKEN_TILES, PASSES * P], U32, align_bytes=64)
         cat_scales = keep.tile([P, TOKEN_TILES, PASSES * P], U8, align_bytes=64)
@@ -126,9 +151,9 @@ def tile_stulayer_pb_kernel(tc, u, attn_out, src_norm, w_out, b_out, ln2_w, ln2_
             )
             issued[(i, h)] = issued[(i, h)] + 1
 
-        def flip_two_passes(rows):
+        def flip_two_passes(rows, bank):
             words = rows.bitcast(F32)
-            flipped = psum.tile([P, 4, P], F32, tag="bank")
+            flipped = psum.tile([P, 4, P], F32, tag=bank)
             for q in range(4):
                 g, h = divmod(q, 2)
                 every_second = words[:, 2 * P * g + h : 2 * P * (g + 1) : 2]
@@ -140,53 +165,86 @@ def tile_stulayer_pb_kernel(tc, u, attn_out, src_norm, w_out, b_out, ln2_w, ln2_
             )
             return grouped
 
-        def flip_tokens(i):
-            flips = [(RES_PASSES, flip_two_passes(src_tiles[i][:]))]
-            for first_pass in range(0, RES_PASSES, 2):
-                cols = slice(first_pass * K_PASS, (first_pass + 2) * K_PASS)
-                residual = stage.tile([P, 2 * K_PASS], BF16, bufs=4)
-                nc.vector.tensor_tensor(
-                    out=residual[:], in0=u_tiles[i][:, cols], in1=attn_tiles[i][:, cols], op=ALU.add
-                )
-                flips.append((first_pass, flip_two_passes(residual[:])))
-            return flips
+        groups = {}
 
-        def quantise_tokens(i, flips):
-            for first_pass, grouped in flips:
-                cols = slice(first_pass * P, (first_pass + 2) * P)
-                nc.vector.quantize_mx(
-                    out=cat_codes[:, i, cols].bitcast(FP8X4), scales=cat_scales[:, i, cols], in_=grouped[:]
-                )
-            accs[i] = [psum.tile([P, BANK], F32, tag="bank", name="acc%d%d" % (i, h)) for h in range(HALVES)]
+        def flip_src(i, bank):
+            groups[(i, RES_PASSES)] = flip_two_passes(src_tiles[i][:], bank)
+
+        residuals = {}
+
+        def add_res(i, c):
+            cols = slice(c * 2 * K_PASS, (c + 1) * 2 * K_PASS)
+            nc.vector.tensor_tensor(
+                out=u_tiles[i][:, cols], in0=u_tiles[i][:, cols], in1=attn_tiles[i][:, cols], op=ALU.add
+            )
+            residuals[(i, c)] = u_tiles[i][:, cols]
+
+        def flip_res_chunk(i, c, bank):
+            groups[(i, 2 * c)] = flip_two_passes(residuals[(i, c)], bank)
+
+        def flip_res(i, banks):
+            for c in range(2):
+                add_res(i, c)
+                flip_res_chunk(i, c, banks[c])
+
+        def quantise_chunk(i, first_pass):
+            cols = slice(first_pass * P, (first_pass + 2) * P)
+            nc.vector.quantize_mx(
+                out=cat_codes[:, i, cols].bitcast(FP8X4), scales=cat_scales[:, i, cols], in_=groups[(i, first_pass)][:]
+            )
+
+        def open_tile(i, banks):
+            accs[i] = [psum.tile([P, BANK], F32, tag=banks[h], name="acc%d%d" % (i, h)) for h in range(HALVES)]
             for h in range(HALVES):
                 issued[(i, h)] = 0
+
+        def join_tile(i, passes=range(PASSES), last=True):
             for g, h in ready_weights:
-                multiply(i, g, h)
-            ready_tiles.append(i)
+                if g in passes:
+                    multiply(i, g, h)
+            if last:
+                ready_tiles.append(i)
 
-        def regroup_weights(g):
-            halves = []
-            for h in range(HALVES):
-                grouped = stage.tile([P, BANK * PACK], BF16, align_bytes=64, name="w_grouped%d" % h)
-                copy = nc.vector.tensor_copy if h == 0 else nc.scalar.copy
+        w_groups = {}
+
+        def columns_of(g, first, last):
+            if g in SPLIT:
+                h = first // BANK
+                return w_raw[g][:, h, :, first - h * BANK : last - h * BANK]
+            return w_raw[g][:, :, first:last]
+
+        def regroup_weights(g, shares):
+            grouped = stage.tile([P, D * PACK], BF16, align_bytes=64, name="w_grouped", bufs=3)
+            for engine, first, last in shares:
+                copy = nc.vector.tensor_copy if engine == "v" else nc.scalar.copy
                 copy(
-                    out=grouped[:].rearrange("p (c i t) -> p c t i", i=4, t=PACK),
-                    in_=w_raw[g][:, :, h * BANK : (h + 1) * BANK].rearrange("p t (c i) -> p c t i", i=4),
+                    out=grouped[:, first * PACK : last * PACK].rearrange("p (c i t) -> p c t i", i=4, t=PACK),
+                    in_=columns_of(g, first, last).rearrange("p t (c i) -> p c t i", i=4),
                 )
-                halves.append(grouped)
-            return halves
+            w_groups[g] = grouped
 
-        def quantise_weights(g, h, grouped):
-            cols = slice(h * BANK, (h + 1) * BANK)
-            nc.vector.quantize_mx(
-                out=w_codes[:, g, cols].bitcast(FP8X4), scales=w_scales[:, g, cols], in_=grouped[:]
-            )
-            for i in ready_tiles:
-                multiply(i, g, h)
-            ready_weights.append((g, h))
+        def quantise_weights(g, halves=((0, 1),)):
+            for hs in halves:
+                cols = slice(hs[0] * BANK, (hs[-1] + 1) * BANK)
+                nc.vector.quantize_mx(
+                    out=w_codes[:, g, cols].bitcast(FP8X4),
+                    scales=w_scales[:, g, cols],
+                    in_=w_groups[g][:, cols.start * PACK : cols.stop * PACK],
+                )
+                for i in ready_tiles:
+                    for h in hs:
+                        multiply(i, g, h)
+                for h in hs:
+                    ready_weights.append((g, h))
 
-        def centre_and_gain(i):
-            z = stage.tile([P, D], F32)
+        zs = {}
+        sums = {}
+        gains = {}
+        rstds = {}
+        shifts = {}
+
+        def add_bias(i):
+            z = stage.tile([P, D], F32, bufs=4)
             z_sum = small.tile([P, HALVES], F32)
             for h in range(HALVES):
                 cols = slice(h * BANK, (h + 1) * BANK)
@@ -199,6 +257,10 @@ def tile_stulayer_pb_kernel(tc, u, attn_out, src_norm, w_out, b_out, ln2_w, ln2_
                     op1=ALU.add,
                     accum_out=z_sum[:, h : h + 1],
                 )
+            sums[i] = (z, z_sum)
+
+        def negate_mean(i):
+            z, z_sum = sums[i]
             neg_mean = small.tile([P, 1], F32)
             nc.vector.tensor_scalar(
                 out=neg_mean[:],
@@ -208,10 +270,13 @@ def tile_stulayer_pb_kernel(tc, u, attn_out, src_norm, w_out, b_out, ln2_w, ln2_
                 op0=ALU.add,
                 op1=ALU.mult,
             )
+            zs[i] = (z, neg_mean)
+
+        def shift(i, banks):
             shifted = []
             for h in range(HALVES):
                 cols = slice(h * BANK, (h + 1) * BANK)
-                shifted_ps = psum.tile([P, BANK], F32, tag="bank", name="shifted%d" % h)
+                shifted_ps = psum.tile([P, BANK], F32, tag=banks[h], name="shifted%d%d" % (i, h))
                 nc.tensor.matmul(
                     out=shifted_ps[:], lhsT=ident_bf16[:], rhs=src_tiles[i][:, cols], start=True, stop=False
                 )
@@ -219,8 +284,11 @@ def tile_stulayer_pb_kernel(tc, u, attn_out, src_norm, w_out, b_out, ln2_w, ln2_
                     out=shifted_ps[:], lhsT=ones[:], rhs=shift_row[:, cols], start=False, stop=True
                 )
                 shifted.append(shifted_ps)
+            shifts[i] = shifted
 
-            gained = stage.tile([P, D], F32, bufs=LAG + 1)
+        def centre(i):
+            z, neg_mean = zs[i]
+            gained = stage.tile([P, D], F32, bufs=4)
             if i < TOKEN_TILES - 1:
                 centred = stage.tile([P, D], F32)
                 nc.scalar.activation(out=centred[:], in_=z[:], func=ACT.Identity, bias=neg_mean[:])
@@ -229,7 +297,10 @@ def tile_stulayer_pb_kernel(tc, u, attn_out, src_norm, w_out, b_out, ln2_w, ln2_
                 nc.vector.scalar_tensor_tensor(
                     out=gained[:], in0=z[:], scalar=neg_mean[:], in1=gain_all[:], op0=ALU.add, op1=ALU.mult
                 )
+            gains[i] = gained
 
+        def spread_of(i):
+            z, neg_mean = zs[i]
             squares = stage.tile([P, D], BF16)
             sq_sum = small.tile([P, 1], F32)
             nc.scalar.activation(
@@ -239,10 +310,11 @@ def tile_stulayer_pb_kernel(tc, u, attn_out, src_norm, w_out, b_out, ln2_w, ln2_
             nc.scalar.activation(
                 out=rstd[:], in_=sq_sum[:], func=ACT.Abs_reciprocal_sqrt, bias=eps[:], scale=1.0 / D
             )
-            return gained, rstd, shifted
+            rstds[i] = rstd
 
-        def scale_and_store(i, gained, rstd, shifted):
-            result = stage.tile([P, D], F32)
+        def scale_and_store(i):
+            gained, rstd, shifted = gains[i], rstds[i], shifts[i]
+            result = stage.tile([P, D], F32, bufs=4)
             for h in range(HALVES):
                 cols = slice(h * BANK, (h + 1) * BANK)
                 nc.vector.scalar_tensor_tensor(
@@ -255,29 +327,85 @@ def tile_stulayer_pb_kernel(tc, u, attn_out, src_norm, w_out, b_out, ln2_w, ln2_
                 )
                 nc.sync.dma_start(out=out_rows[i * P : (i + 1) * P, cols], in_=result[:, cols])
 
-        flips = {}
-        waiting = None
-        for n, g in enumerate(PASS_ORDER):
-            halves = regroup_weights(g)
-            if waiting is not None:
-                quantise_weights(waiting[0], 1, waiting[1])
-            quantise_weights(g, 0, halves[0])
-            waiting = (g, halves[1])
-            if 0 <= n - 1 < EARLY_TILES:
-                quantise_tokens(n - 1, flips[n - 1])
-            if n < EARLY_TILES:
-                flips[n] = flip_tokens(n)
-        quantise_weights(waiting[0], 1, waiting[1])
-
-        ends = {}
-        for i in range(TOKEN_TILES):
-            late = i + EARLY_TILES
-            if late < TOKEN_TILES:
-                flips[late] = flip_tokens(late)
-            if EARLY_TILES <= late - 1 < TOKEN_TILES:
-                quantise_tokens(late - 1, flips[late - 1])
-            if i >= LAG:
-                scale_and_store(i - LAG, *ends[i - LAG])
-            ends[i] = centre_and_gain(i)
-        for i in range(TOKEN_TILES - LAG, TOKEN_TILES):
-            scale_and_store(i, *ends[i])
+        A, B, C, T = ("a0", "a1"), ("b0", "b1"), ("c0", "c1"), ("t0", "t1")
+        regroup_weights(4, (("v", 0, BANK), ("v", BANK, D)))
+        quantise_weights(4, ((0,),))
+        spread(0, bias_all, "c0")
+        spread(8, gain_all, "c1")
+        regroup_weights(5, (("v", 0, 480), ("s", 480, D)))
+        quantise_weights(4, ((1,),))
+        flip_src(0, "t1")
+        add_res(0, 0)
+        add_res(0, 1)
+        flip_res_chunk(0, 0, "t0")
+        flip_res_chunk(0, 1, "c0")
+        quantise_weights(5)
+        regroup_weights(0, (("v", 0, 480), ("s", 480, D)))
+        open_tile(0, A)
+        quantise_chunk(0, 4)
+        quantise_chunk(0, 0)
+        quantise_chunk(0, 2)
+        join_tile(0)
+        flip_src(1, "c1")
+        add_res(1, 0)
+        add_res(1, 1)
+        flip_res_chunk(1, 0, "t1")
+        flip_res_chunk(1, 1, "t0")
+        quantise_weights(0)
+        regroup_weights(1, (("v", 0, 480), ("s", 480, D)))
+        open_tile(1, B)
+        quantise_chunk(1, 4)
+        quantise_chunk(1, 0)
+        quantise_chunk(1, 2)
+        join_tile(1)
+        flip_src(2, "t1")
+        add_res(2, 0)
+        add_res(2, 1)
+        flip_res_chunk(2, 0, "t0")
+        flip_res_chunk(2, 1, "t1")
+        quantise_weights(1)
+        regroup_weights(2, (("v", 0, 480), ("s", 480, D)))
+        open_tile(2, C)
+        quantise_chunk(2, 4)
+        quantise_chunk(2, 0)
+        quantise_chunk(2, 2)
+        join_tile(2)
+        regroup_weights(3, (("v", 0, 256), ("s", 0 + 256, BANK), ("v", BANK, 768), ("s", 768, D)))
+        quantise_weights(2)
+        add_res(3, 0)
+        quantise_weights(3, ((0,),))
+        add_res(3, 1)
+        quantise_weights(3, ((1,),))
+        flip_src(3, "t0")
+        flip_res_chunk(3, 0, "t1")
+        flip_res_chunk(3, 1, "t0")
+        add_bias(0)
+        negate_mean(0)
+        centre(0)
+        quantise_chunk(3, 4)
+        open_tile(3, A)
+        join_tile(3, (4, 5), False)
+        add_bias(1)
+        negate_mean(1)
+        centre(1)
+        quantise_chunk(3, 0)
+        quantise_chunk(3, 2)
+        shift(0, B)
+        join_tile(3, (0, 1, 2, 3))
+        spread_of(0)
+        add_bias(2)
+        negate_mean(2)
+        centre(2)
+        spread_of(1)
+        shift(1, T)
+        shift(2, C)
+        scale_and_store(0)
+        add_bias(3)
+        negate_mean(3)
+        spread_of(2)
+        spread_of(3)
+        shift(3, A)
+        scale_and_store(1)
+        centre(3)
+        scale_and_store(2)
+        scale_and_store(3)

@@ -26,7 +26,7 @@ PASSES = K // K_PASS
 RES_PASSES = RES // K_PASS
 HALVES = D // BANK
 
-SPLIT = (3, 4)
+SPLIT = ()
 FLOPS = 2 * TOKENS * K * D
 
 
@@ -85,25 +85,23 @@ def tile_stulayer_pb_kernel(tc, u, attn_out, src_norm, w_out, b_out, ln2_w, ln2_
                     in_=w_out[g * K_PASS : (g + 1) * K_PASS, cols].rearrange("(p t) c -> p t c", t=PACK),
                 )
 
-        load_w_part(4, 0)
+        load_weights(4)
         nc.sync.dma_start(out=vec_rows[0:8, :], in_=b_out.rearrange("(r c) -> r c", c=P))
         nc.sync.dma_start(out=vec_rows[8:16, :], in_=ln2_w.rearrange("(r c) -> r c", c=P))
-        load_w_part(4, 1)
         load_weights(5)
         load_src(0)
         load_residual(0)
         nc.sync.dma_start(out=shift_row[0:1, :], in_=ln2_b.rearrange("(o c) -> o c", o=1))
         load_weights(0)
+        load_weights(1)
         load_src(1)
         load_residual(1)
-        load_weights(1)
-        load_src(2)
-        load_residual(2)
         load_weights(2)
-        load_w_part(3, 0)
-        load_w_part(3, 1)
+        load_src(2)
+        load_weights(3)
+        load_residual(2)
         load_src(3)
-        load_residual(3, parts=2)
+        load_residual(3)
 
         warm = keep.tile([P, 1], F32)
         nc.scalar.activation(out=warm[:], in_=eps[:], func=ACT.Abs_reciprocal_sqrt)
@@ -139,6 +137,11 @@ def tile_stulayer_pb_kernel(tc, u, attn_out, src_norm, w_out, b_out, ln2_w, ln2_
         issued = {}
 
         def multiply(i, g, h):
+            if i not in accs:
+                banks = (("a0", "a1"), ("b0", "b1"), ("c0", "c1"), ("a0", "a1"))[i]
+                accs[i] = [psum.tile([P, BANK], F32, tag=banks[h2], name="acc%d%d" % (i, h2)) for h2 in range(HALVES)]
+                for h2 in range(HALVES):
+                    issued[(i, h2)] = 0
             cols = slice(h * BANK, (h + 1) * BANK)
             nc.tensor.matmul_mx(
                 out=accs[i][h][:],
@@ -151,13 +154,16 @@ def tile_stulayer_pb_kernel(tc, u, attn_out, src_norm, w_out, b_out, ln2_w, ln2_
             )
             issued[(i, h)] = issued[(i, h)] + 1
 
-        def flip_two_passes(rows, bank):
+        def turn(rows, bank):
             words = rows.bitcast(F32)
-            flipped = psum.tile([P, 4, P], F32, tag=bank)
+            flipped = psum.tile([P, 4, P], F32, tag=bank, name="flipped")
             for q in range(4):
                 g, h = divmod(q, 2)
                 every_second = words[:, 2 * P * g + h : 2 * P * (g + 1) : 2]
                 nc.tensor.transpose(flipped[:, q, :], every_second, ident_f32[:])
+            return flipped
+
+        def empty(flipped):
             grouped = stage.tile([P, 2 * K_PASS], BF16, align_bytes=64, name="cat_grouped", bufs=6)
             nc.scalar.copy(
                 out=grouped[:].bitcast(F32).rearrange("p (g t h) -> p g t h", t=P, h=2),
@@ -165,27 +171,36 @@ def tile_stulayer_pb_kernel(tc, u, attn_out, src_norm, w_out, b_out, ln2_w, ln2_
             )
             return grouped
 
-        groups = {}
+        turned = {}
 
-        def flip_src(i, bank):
-            groups[(i, RES_PASSES)] = flip_two_passes(src_tiles[i][:], bank)
+        def turn_src(i, bank):
+            turned[(i, RES_PASSES)] = turn(src_tiles[i][:], bank)
+
+        groups = {}
 
         residuals = {}
 
         def add_res(i, c):
-            cols = slice(c * 2 * K_PASS, (c + 1) * 2 * K_PASS)
-            nc.vector.tensor_tensor(
-                out=u_tiles[i][:, cols], in0=u_tiles[i][:, cols], in1=attn_tiles[i][:, cols], op=ALU.add
-            )
-            residuals[(i, c)] = u_tiles[i][:, cols]
+            residual = stage.tile([P, 2, K_PASS], BF16, bufs=4)
+            for g in range(2):
+                cols = slice((2 * c + g) * K_PASS, (2 * c + g + 1) * K_PASS)
+                nc.vector.tensor_tensor(
+                    out=residual[:, g].rearrange("q (h p e) -> q h p e", h=2, e=2),
+                    in0=u_tiles[i][:, cols].rearrange("q (p h e) -> q h p e", h=2, e=2),
+                    in1=attn_tiles[i][:, cols].rearrange("q (p h e) -> q h p e", h=2, e=2),
+                    op=ALU.add,
+                )
+            residuals[(i, c)] = residual
 
-        def flip_res_chunk(i, c, bank):
-            groups[(i, 2 * c)] = flip_two_passes(residuals[(i, c)], bank)
+        def turn_res(i, c, bank):
+            words = residuals[(i, c)][:].rearrange("q g f -> q (g f)").bitcast(F32)
+            flipped = psum.tile([P, 4, P], F32, tag=bank, name="flipped")
+            for q in range(4):
+                nc.tensor.transpose(flipped[:, q, :], words[:, q * P : (q + 1) * P], ident_f32[:])
+            turned[(i, 2 * c)] = flipped
 
-        def flip_res(i, banks):
-            for c in range(2):
-                add_res(i, c)
-                flip_res_chunk(i, c, banks[c])
+        def empty_chunk(i, first_pass):
+            groups[(i, first_pass)] = empty(turned[(i, first_pass)])
 
         def quantise_chunk(i, first_pass):
             cols = slice(first_pass * P, (first_pass + 2) * P)
@@ -193,15 +208,11 @@ def tile_stulayer_pb_kernel(tc, u, attn_out, src_norm, w_out, b_out, ln2_w, ln2_
                 out=cat_codes[:, i, cols].bitcast(FP8X4), scales=cat_scales[:, i, cols], in_=groups[(i, first_pass)][:]
             )
 
-        def open_tile(i, banks):
-            accs[i] = [psum.tile([P, BANK], F32, tag=banks[h], name="acc%d%d" % (i, h)) for h in range(HALVES)]
-            for h in range(HALVES):
-                issued[(i, h)] = 0
-
         def join_tile(i, passes=range(PASSES), last=True):
-            for g, h in ready_weights:
-                if g in passes:
-                    multiply(i, g, h)
+            for h in range(HALVES):
+                for g, h2 in ready_weights:
+                    if g in passes and h2 == h:
+                        multiply(i, g, h)
             if last:
                 ready_tiles.append(i)
 
@@ -244,6 +255,7 @@ def tile_stulayer_pb_kernel(tc, u, attn_out, src_norm, w_out, b_out, ln2_w, ln2_
         shifts = {}
 
         def add_bias(i):
+            assert all(issued[(i, h)] == PASSES for h in range(HALVES))
             z = stage.tile([P, D], F32, bufs=4)
             z_sum = small.tile([P, HALVES], F32)
             for h in range(HALVES):
@@ -262,14 +274,8 @@ def tile_stulayer_pb_kernel(tc, u, attn_out, src_norm, w_out, b_out, ln2_w, ln2_
         def negate_mean(i):
             z, z_sum = sums[i]
             neg_mean = small.tile([P, 1], F32)
-            nc.vector.tensor_scalar(
-                out=neg_mean[:],
-                in0=z_sum[:, 0:1],
-                scalar1=z_sum[:, 1:2],
-                scalar2=-1.0 / D,
-                op0=ALU.add,
-                op1=ALU.mult,
-            )
+            scaled = small.tile([P, HALVES], F32)
+            nc.scalar.activation(out=scaled[:], in_=z_sum[:], func=ACT.Identity, scale=-1.0 / D, accum_out=neg_mean[:])
             zs[i] = (z, neg_mean)
 
         def shift(i, banks):
@@ -288,7 +294,7 @@ def tile_stulayer_pb_kernel(tc, u, attn_out, src_norm, w_out, b_out, ln2_w, ln2_
 
         def centre(i):
             z, neg_mean = zs[i]
-            gained = stage.tile([P, D], F32, bufs=4)
+            gained = stage.tile([P, D], F32, bufs=3)
             if i < TOKEN_TILES - 1:
                 centred = stage.tile([P, D], F32)
                 nc.scalar.activation(out=centred[:], in_=z[:], func=ACT.Identity, bias=neg_mean[:])
@@ -314,7 +320,7 @@ def tile_stulayer_pb_kernel(tc, u, attn_out, src_norm, w_out, b_out, ln2_w, ln2_
 
         def scale_and_store(i):
             gained, rstd, shifted = gains[i], rstds[i], shifts[i]
-            result = stage.tile([P, D], F32, bufs=4)
+            result = stage.tile([P, D], F32, bufs=3)
             for h in range(HALVES):
                 cols = slice(h * BANK, (h + 1) * BANK)
                 nc.vector.scalar_tensor_tensor(
@@ -328,84 +334,90 @@ def tile_stulayer_pb_kernel(tc, u, attn_out, src_norm, w_out, b_out, ln2_w, ln2_
                 nc.sync.dma_start(out=out_rows[i * P : (i + 1) * P, cols], in_=result[:, cols])
 
         A, B, C, T = ("a0", "a1"), ("b0", "b1"), ("c0", "c1"), ("t0", "t1")
-        regroup_weights(4, (("v", 0, BANK), ("v", BANK, D)))
-        quantise_weights(4, ((0,),))
+        regroup_weights(4, (("v", 0, 512), ("s", 512, D)))
+        regroup_weights(5, (("v", 0, 512), ("s", 512, D)))
+        quantise_weights(4)
+        turn_src(0, "t1")
+        add_res(0, 0)
+        empty_chunk(0, 4)
+        add_res(0, 1)
         spread(0, bias_all, "c0")
         spread(8, gain_all, "c1")
-        regroup_weights(5, (("v", 0, 480), ("s", 480, D)))
-        quantise_weights(4, ((1,),))
-        flip_src(0, "t1")
-        add_res(0, 0)
-        add_res(0, 1)
-        flip_res_chunk(0, 0, "t0")
-        flip_res_chunk(0, 1, "c0")
         quantise_weights(5)
-        regroup_weights(0, (("v", 0, 480), ("s", 480, D)))
-        open_tile(0, A)
+        turn_res(0, 0, "t0")
+        empty_chunk(0, 0)
+        turn_res(0, 1, "t1")
+        regroup_weights(0, (("v", 0, 512), ("s", 512, D)))
+        empty_chunk(0, 2)
         quantise_chunk(0, 4)
         quantise_chunk(0, 0)
-        quantise_chunk(0, 2)
         join_tile(0)
-        flip_src(1, "c1")
+        regroup_weights(1, (("v", 0, 512), ("s", 512, D)))
+        turn_src(1, "c1")
+        quantise_weights(0)
         add_res(1, 0)
         add_res(1, 1)
-        flip_res_chunk(1, 0, "t1")
-        flip_res_chunk(1, 1, "t0")
-        quantise_weights(0)
-        regroup_weights(1, (("v", 0, 480), ("s", 480, D)))
-        open_tile(1, B)
+        turn_res(1, 0, "c0")
+        turn_res(1, 1, "t0")
+        empty_chunk(1, 4)
+        empty_chunk(1, 0)
+        empty_chunk(1, 2)
+        quantise_chunk(0, 2)
+        quantise_weights(1)
+        regroup_weights(2, (("v", 0, 512), ("s", 512, D)))
         quantise_chunk(1, 4)
         quantise_chunk(1, 0)
         quantise_chunk(1, 2)
         join_tile(1)
-        flip_src(2, "t1")
+        regroup_weights(3, (("v", 0, 512), ("s", 512, D)))
+        turn_src(2, "t1")
+        empty_chunk(2, 4)
+        quantise_weights(2)
+        quantise_weights(3)
         add_res(2, 0)
         add_res(2, 1)
-        flip_res_chunk(2, 0, "t0")
-        flip_res_chunk(2, 1, "t1")
-        quantise_weights(1)
-        regroup_weights(2, (("v", 0, 480), ("s", 480, D)))
-        open_tile(2, C)
+        turn_res(2, 0, "t0")
+        empty_chunk(2, 0)
+        turn_res(2, 1, "t1")
+        empty_chunk(2, 2)
         quantise_chunk(2, 4)
-        quantise_chunk(2, 0)
-        quantise_chunk(2, 2)
-        join_tile(2)
-        regroup_weights(3, (("v", 0, 256), ("s", 0 + 256, BANK), ("v", BANK, 768), ("s", 768, D)))
-        quantise_weights(2)
-        add_res(3, 0)
-        quantise_weights(3, ((0,),))
-        add_res(3, 1)
-        quantise_weights(3, ((1,),))
-        flip_src(3, "t0")
-        flip_res_chunk(3, 0, "t1")
-        flip_res_chunk(3, 1, "t0")
+        join_tile(2, (4, 5), False)
         add_bias(0)
         negate_mean(0)
+        add_res(3, 0)
+        quantise_chunk(2, 0)
+        quantise_chunk(2, 2)
         centre(0)
-        quantise_chunk(3, 4)
-        open_tile(3, A)
-        join_tile(3, (4, 5), False)
+        turn_src(3, "t0")
+        empty_chunk(3, 4)
+        turn_res(3, 0, "t1")
+        empty_chunk(3, 0)
+        add_res(3, 1)
+        join_tile(2, (0, 1, 2, 3))
+        turn_res(3, 1, "t0")
+        spread_of(0)
+        empty_chunk(3, 2)
         add_bias(1)
         negate_mean(1)
-        centre(1)
+        quantise_chunk(3, 4)
+        add_bias(2)
         quantise_chunk(3, 0)
         quantise_chunk(3, 2)
         shift(0, B)
-        join_tile(3, (0, 1, 2, 3))
-        spread_of(0)
-        add_bias(2)
+        centre(1)
         negate_mean(2)
+        join_tile(3)
+        scale_and_store(0)
         centre(2)
         spread_of(1)
         shift(1, T)
-        shift(2, C)
-        scale_and_store(0)
         add_bias(3)
-        negate_mean(3)
         spread_of(2)
+        negate_mean(3)
         spread_of(3)
-        shift(3, A)
+        shift(3, B)
         scale_and_store(1)
         centre(3)
+        shift(2, C)
         scale_and_store(2)
         scale_and_store(3)

@@ -97,8 +97,8 @@ def tile_stulayer_pb_kernel(tc, u, attn_out, src_norm, w_out, b_out, ln2_w, ln2_
         load_src(1)
         load_residual(1)
         load_weights(2)
-        load_src(2)
         load_weights(3)
+        load_src(2)
         load_residual(2)
         load_src(3)
         load_residual(3)
@@ -399,8 +399,8 @@ def tile_stulayer_pb_kernel(tc, u, attn_out, src_norm, w_out, b_out, ln2_w, ln2_
         empty_chunk(3, 2)
         add_bias(1)
         negate_mean(1)
-        quantise_chunk(3, 4)
         add_bias(2)
+        quantise_chunk(3, 4)
         quantise_chunk(3, 0)
         quantise_chunk(3, 2)
         shift(0, B)

from contextlib import ExitStack

import concourse.mybir as mybir
from concourse.masks import make_identity

F32 = mybir.dt.float32
BF16 = mybir.dt.bfloat16
U32 = mybir.dt.uint32
U8 = mybir.dt.uint8
FP8X4 = mybir.dt.float8_e4m3fn_x4
ALU = mybir.AluOpType
ACT = mybir.ActivationFunctionType

P = 128
PACK = 4
K_PASS = P * PACK
TOKENS = 512
RES = 2048
D = 1024
K = RES + D
BANK = 512
EPS = 1e-5

TOKEN_TILES = TOKENS // P
PASSES = K // K_PASS
RES_PASSES = RES // K_PASS
HALVES = D // BANK

SPLIT = ()
FLOPS = 2 * TOKENS * K * D


def tile_stulayer_pb_kernel(tc, u, attn_out, src_norm, w_out, b_out, ln2_w, ln2_b, out):
    nc = tc.nc
    u_rows = u.rearrange("t b f -> (t b) f")
    attn_rows = attn_out.rearrange("t b f -> (t b) f")
    src_rows = src_norm.rearrange("t b f -> (t b) f")
    out_rows = out.rearrange("t b f -> (t b) f")

    with ExitStack() as ctx:
        ctx.enter_context(tc.manual_schedule())
        keep = ctx.enter_context(tc.tile_pool(name="keep", bufs=1))
        stage = ctx.enter_context(tc.tile_pool(name="stage", bufs=2))
        small = ctx.enter_context(tc.tile_pool(name="small", bufs=TOKEN_TILES))
        psum = ctx.enter_context(tc.psum_pool(name="psum", bufs=1))

        vec_rows = keep.tile([P, P], BF16)
        nc.vector.memset(vec_rows[:], 0.0)
        shift_row = keep.tile([P, D], BF16)
        nc.vector.memset(shift_row[:], 0.0)
        eps = keep.tile([P, 1], F32)
        nc.vector.memset(eps[:], EPS)
        ones = keep.tile([P, P], BF16)
        nc.vector.memset(ones[:], 1.0)

        u_tiles = [keep.tile([P, RES], BF16, name="u%d" % i) for i in range(TOKEN_TILES)]
        attn_tiles = [keep.tile([P, RES], BF16, name="attn%d" % i) for i in range(TOKEN_TILES)]
        src_tiles = [keep.tile([P, D], BF16, name="src%d" % i) for i in range(TOKEN_TILES)]
        w_raw = [keep.tile([P, HALVES, PACK, BANK] if g in SPLIT else [P, PACK, D], BF16, name="w_raw%d" % g) for g in range(PASSES)]

        def load_src(i):
            nc.sync.dma_start(out=src_tiles[i][:], in_=src_rows[i * P : (i + 1) * P, :])

        def load_residual(i, parts=1):
            rows = slice(i * P, (i + 1) * P)
            width = RES // parts
            for c in range(parts):
                cols = slice(c * width, (c + 1) * width)
                nc.sync.dma_start(out=u_tiles[i][:, cols], in_=u_rows[rows, cols])
                nc.sync.dma_start(out=attn_tiles[i][:, cols], in_=attn_rows[rows, cols])

        def load_w_part(g, h):
            cols = slice(h * BANK, (h + 1) * BANK)
            nc.sync.dma_start(
                out=w_raw[g][:, h],
                in_=w_out[g * K_PASS : (g + 1) * K_PASS, cols].rearrange("(p t) c -> p t c", t=PACK),
            )

        def load_weights(g, parts=1):
            width = D // parts
            for c in range(parts):
                cols = slice(c * width, (c + 1) * width)
                nc.sync.dma_start(
                    out=w_raw[g][:, :, cols],
                    in_=w_out[g * K_PASS : (g + 1) * K_PASS, cols].rearrange("(p t) c -> p t c", t=PACK),
                )

        load_weights(4)
        nc.sync.dma_start(out=vec_rows[0:8, :], in_=b_out.rearrange("(r c) -> r c", c=P))
        nc.sync.dma_start(out=vec_rows[8:16, :], in_=ln2_w.rearrange("(r c) -> r c", c=P))
        load_weights(5)
        load_src(0)
        load_residual(0)
        nc.sync.dma_start(out=shift_row[0:1, :], in_=ln2_b.rearrange("(o c) -> o c", o=1))
        load_weights(0)
        load_weights(1)
        load_src(1)
        load_residual(1)
        load_weights(2)
        load_weights(3)
        load_src(2)
        load_residual(2)
        load_src(3)
        load_residual(3)

        warm = keep.tile([P, 1], F32)
        nc.scalar.activation(out=warm[:], in_=eps[:], func=ACT.Abs_reciprocal_sqrt)
        ident_bf16 = keep.tile([P, P], BF16)
        make_identity(nc, ident_bf16[:])
        ident_f32 = keep.tile([P, P], F32)
        make_identity(nc, ident_f32[:])

        vec_cols_ps = psum.tile([P, P], BF16, tag="t0")
        nc.tensor.transpose(vec_cols_ps[:], vec_rows[:], ident_bf16[:])
        vec_cols = keep.tile([P, P], BF16)
        nc.scalar.copy(out=vec_cols[:], in_=vec_cols_ps[:])
        bias_all = keep.tile([P, D], BF16)
        gain_all = keep.tile([P, D], BF16)

        def spread(first_row, target, bank):
            spread_ps = psum.tile([P, D], BF16, tag=bank)
            for r in range(D // P):
                column = vec_cols[:, first_row + r : first_row + r + 1]
                nc.tensor.transpose(
                    spread_ps[:, r * P : (r + 1) * P], column.to_broadcast([P, P]), ident_bf16[:]
                )
            nc.scalar.copy(out=target[:], in_=spread_ps[:])

        cat_codes = keep.tile([P, TOKEN_TILES, PASSES * P], U32, align_bytes=64)
        cat_scales = keep.tile([P, TOKEN_TILES, PASSES * P], U8, align_bytes=64)
        w_codes = keep.tile([P, PASSES, D], U32, align_bytes=64)
        w_scales = keep.tile([P, PASSES, D], U8, align_bytes=64)

        ready_tiles = []
        ready_weights = []
        accs = {}
        issued = {}

        def multiply(i, g, h):
            if i not in accs:
                banks = (("a0", "a1"), ("b0", "b1"), ("c0", "c1"), ("a0", "a1"))[i]
                accs[i] = [psum.tile([P, BANK], F32, tag=banks[h2], name="acc%d%d" % (i, h2)) for h2 in range(HALVES)]
                for h2 in range(HALVES):
                    issued[(i, h2)] = 0
            cols = slice(h * BANK, (h + 1) * BANK)
            nc.tensor.matmul_mx(
                out=accs[i][h][:],
                lhsT=cat_codes[:, i, g * P : (g + 1) * P].bitcast(FP8X4),
                lhsT_scale=cat_scales[:, i, g * P : (g + 1) * P],
                rhs=w_codes[:, g, cols].bitcast(FP8X4),
                rhs_scale=w_scales[:, g, cols],
                start=(issued[(i, h)] == 0),
                stop=(issued[(i, h)] == PASSES - 1),
            )
            issued[(i, h)] = issued[(i, h)] + 1

        def turn(rows, bank):
            words = rows.bitcast(F32)
            flipped = psum.tile([P, 4, P], F32, tag=bank, name="flipped")
            for q in range(4):
                g, h = divmod(q, 2)
                every_second = words[:, 2 * P * g + h : 2 * P * (g + 1) : 2]
                nc.tensor.transpose(flipped[:, q, :], every_second, ident_f32[:])
            return flipped

        def empty(flipped):
            grouped = stage.tile([P, 2 * K_PASS], BF16, align_bytes=64, name="cat_grouped", bufs=6)
            nc.scalar.copy(
                out=grouped[:].bitcast(F32).rearrange("p (g t h) -> p g t h", t=P, h=2),
                in_=flipped[:].rearrange("p (g h) t -> p g t h", h=2),
            )
            return grouped

        turned = {}

        def turn_src(i, bank):
            turned[(i, RES_PASSES)] = turn(src_tiles[i][:], bank)

        groups = {}

        residuals = {}

        def add_res(i, c):
            residual = stage.tile([P, 2, K_PASS], BF16, bufs=4)
            for g in range(2):
                cols = slice((2 * c + g) * K_PASS, (2 * c + g + 1) * K_PASS)
                nc.vector.tensor_tensor(
                    out=residual[:, g].rearrange("q (h p e) -> q h p e", h=2, e=2),
                    in0=u_tiles[i][:, cols].rearrange("q (p h e) -> q h p e", h=2, e=2),
                    in1=attn_tiles[i][:, cols].rearrange("q (p h e) -> q h p e", h=2, e=2),
                    op=ALU.add,
                )
            residuals[(i, c)] = residual

        def turn_res(i, c, bank):
            words = residuals[(i, c)][:].rearrange("q g f -> q (g f)").bitcast(F32)
            flipped = psum.tile([P, 4, P], F32, tag=bank, name="flipped")
            for q in range(4):
                nc.tensor.transpose(flipped[:, q, :], words[:, q * P : (q + 1) * P], ident_f32[:])
            turned[(i, 2 * c)] = flipped

        def empty_chunk(i, first_pass):
            groups[(i, first_pass)] = empty(turned[(i, first_pass)])

        def quantise_chunk(i, first_pass):
            cols = slice(first_pass * P, (first_pass + 2) * P)
            nc.vector.quantize_mx(
                out=cat_codes[:, i, cols].bitcast(FP8X4), scales=cat_scales[:, i, cols], in_=groups[(i, first_pass)][:]
            )

        def join_tile(i, passes=range(PASSES), last=True):
            for h in range(HALVES):
                for g, h2 in ready_weights:
                    if g in passes and h2 == h:
                        multiply(i, g, h)
            if last:
                ready_tiles.append(i)

        w_groups = {}

        def columns_of(g, first, last):
            if g in SPLIT:
                h = first // BANK
                return w_raw[g][:, h, :, first - h * BANK : last - h * BANK]
            return w_raw[g][:, :, first:last]

        def regroup_weights(g, shares):
            grouped = stage.tile([P, D * PACK], BF16, align_bytes=64, name="w_grouped", bufs=3)
            for engine, first, last in shares:
                copy = nc.vector.tensor_copy if engine == "v" else nc.scalar.copy
                copy(
                    out=grouped[:, first * PACK : last * PACK].rearrange("p (c i t) -> p c t i", i=4, t=PACK),
                    in_=columns_of(g, first, last).rearrange("p t (c i) -> p c t i", i=4),
                )
            w_groups[g] = grouped

        def quantise_weights(g, halves=((0, 1),)):
            for hs in halves:
                cols = slice(hs[0] * BANK, (hs[-1] + 1) * BANK)
                nc.vector.quantize_mx(
                    out=w_codes[:, g, cols].bitcast(FP8X4),
                    scales=w_scales[:, g, cols],
                    in_=w_groups[g][:, cols.start * PACK : cols.stop * PACK],
                )
                for i in ready_tiles:
                    for h in hs:
                        multiply(i, g, h)
                for h in hs:
                    ready_weights.append((g, h))

        zs = {}
        sums = {}
        gains = {}
        rstds = {}
        shifts = {}

        def add_bias(i):
            assert all(issued[(i, h)] == PASSES for h in range(HALVES))
            z = stage.tile([P, D], F32, bufs=4)
            z_sum = small.tile([P, HALVES], F32)
            for h in range(HALVES):
                cols = slice(h * BANK, (h + 1) * BANK)
                nc.vector.scalar_tensor_tensor(
                    out=z[:, cols],
                    in0=accs[i][h][:],
                    scalar=1.0,
                    in1=bias_all[:, cols],
                    op0=ALU.mult,
                    op1=ALU.add,
                    accum_out=z_sum[:, h : h + 1],
                )
            sums[i] = (z, z_sum)

        def negate_mean(i):
            z, z_sum = sums[i]
            neg_mean = small.tile([P, 1], F32)
            scaled = small.tile([P, HALVES], F32)
            nc.scalar.activation(out=scaled[:], in_=z_sum[:], func=ACT.Identity, scale=-1.0 / D, accum_out=neg_mean[:])
            zs[i] = (z, neg_mean)

        def shift(i, banks):
            shifted = []
            for h in range(HALVES):
                cols = slice(h * BANK, (h + 1) * BANK)
                shifted_ps = psum.tile([P, BANK], F32, tag=banks[h], name="shifted%d%d" % (i, h))
                nc.tensor.matmul(
                    out=shifted_ps[:], lhsT=ident_bf16[:], rhs=src_tiles[i][:, cols], start=True, stop=False
                )
                nc.tensor.matmul(
                    out=shifted_ps[:], lhsT=ones[:], rhs=shift_row[:, cols], start=False, stop=True
                )
                shifted.append(shifted_ps)
            shifts[i] = shifted

        def centre(i):
            z, neg_mean = zs[i]
            gained = stage.tile([P, D], F32, bufs=3)
            if i < TOKEN_TILES - 1:
                centred = stage.tile([P, D], F32)
                nc.scalar.activation(out=centred[:], in_=z[:], func=ACT.Identity, bias=neg_mean[:])
                nc.gpsimd.tensor_tensor(out=gained[:], in0=centred[:], in1=gain_all[:], op=ALU.mult)
            else:
                nc.vector.scalar_tensor_tensor(
                    out=gained[:], in0=z[:], scalar=neg_mean[:], in1=gain_all[:], op0=ALU.add, op1=ALU.mult
                )
            gains[i] = gained

        def spread_of(i):
            z, neg_mean = zs[i]
            squares = stage.tile([P, D], BF16)
            sq_sum = small.tile([P, 1], F32)
            nc.scalar.activation(
                out=squares[:], in_=z[:], func=ACT.Square, bias=neg_mean[:], accum_out=sq_sum[:]
            )
            rstd = small.tile([P, 1], F32)
            nc.scalar.activation(
                out=rstd[:], in_=sq_sum[:], func=ACT.Abs_reciprocal_sqrt, bias=eps[:], scale=1.0 / D
            )
            rstds[i] = rstd

        def scale_and_store(i):
            gained, rstd, shifted = gains[i], rstds[i], shifts[i]
            result = stage.tile([P, D], F32, bufs=3)
            for h in range(HALVES):
                cols = slice(h * BANK, (h + 1) * BANK)
                nc.vector.scalar_tensor_tensor(
                    out=result[:, cols],
                    in0=gained[:, cols],
                    scalar=rstd[:],
                    in1=shifted[h][:],
                    op0=ALU.mult,
                    op1=ALU.add,
                )
                nc.sync.dma_start(out=out_rows[i * P : (i + 1) * P, cols], in_=result[:, cols])

        A, B, C, T = ("a0", "a1"), ("b0", "b1"), ("c0", "c1"), ("t0", "t1")
        regroup_weights(4, (("v", 0, 512), ("s", 512, D)))
        regroup_weights(5, (("v", 0, 512), ("s", 512, D)))
        quantise_weights(4)
        turn_src(0, "t1")
        add_res(0, 0)
        empty_chunk(0, 4)
        add_res(0, 1)
        spread(0, bias_all, "c0")
        spread(8, gain_all, "c1")
        quantise_weights(5)
        turn_res(0, 0, "t0")
        empty_chunk(0, 0)
        turn_res(0, 1, "t1")
        regroup_weights(0, (("v", 0, 512), ("s", 512, D)))
        empty_chunk(0, 2)
        quantise_chunk(0, 4)
        quantise_chunk(0, 0)
        join_tile(0)
        regroup_weights(1, (("v", 0, 512), ("s", 512, D)))
        turn_src(1, "c1")
        quantise_weights(0)
        add_res(1, 0)
        add_res(1, 1)
        turn_res(1, 0, "c0")
        turn_res(1, 1, "t0")
        empty_chunk(1, 4)
        empty_chunk(1, 0)
        empty_chunk(1, 2)
        quantise_chunk(0, 2)
        quantise_weights(1)
        regroup_weights(2, (("v", 0, 512), ("s", 512, D)))
        quantise_chunk(1, 4)
        quantise_chunk(1, 0)
        quantise_chunk(1, 2)
        join_tile(1)
        regroup_weights(3, (("v", 0, 512), ("s", 512, D)))
        turn_src(2, "t1")
        empty_chunk(2, 4)
        quantise_weights(2)
        quantise_weights(3)
        add_res(2, 0)
        add_res(2, 1)
        turn_res(2, 0, "t0")
        empty_chunk(2, 0)
        turn_res(2, 1, "t1")
        empty_chunk(2, 2)
        quantise_chunk(2, 4)
        join_tile(2, (4, 5), False)
        add_bias(0)
        negate_mean(0)
        add_res(3, 0)
        quantise_chunk(2, 0)
        quantise_chunk(2, 2)
        centre(0)
        turn_src(3, "t0")
        empty_chunk(3, 4)
        turn_res(3, 0, "t1")
        empty_chunk(3, 0)
        add_res(3, 1)
        join_tile(2, (0, 1, 2, 3))
        turn_res(3, 1, "t0")
        spread_of(0)
        empty_chunk(3, 2)
        add_bias(1)
        negate_mean(1)
        add_bias(2)
        quantise_chunk(3, 4)
        quantise_chunk(3, 0)
        quantise_chunk(3, 2)
        shift(0, B)
        centre(1)
        negate_mean(2)
        join_tile(3)
        scale_and_store(0)
        centre(2)
        spread_of(1)
        shift(1, T)
        add_bias(3)
        spread_of(2)
        negate_mean(3)
        spread_of(3)
        shift(3, B)
        scale_and_store(1)
        centre(3)
        shift(2, C)
        scale_and_store(2)
        scale_and_store(3)
